import numpy as np
import ml_dtypes

BF16 = ml_dtypes.bfloat16


def bf(x):
    return np.asarray(x, np.float32).astype(BF16)


def f32(x):
    return np.asarray(x, np.float32)


def f64(x):
    return np.asarray(x).astype(np.float64)


def striped(idx):
    return np.tile(idx.reshape(-1, 16).T, (8, 1))


P, D, S, H, K, N = 4, 512, 256, 128, 8, 1024
SCALE, SHARE = 0.2, 0.5


def setup_inputs():
    mu = SHARE * np.random.standard_normal((D, 1))
    x = f32(SCALE * (mu[None] + np.random.standard_normal((P, D, S))))
    anchor = f32(SCALE * (mu + np.random.standard_normal((D, N))))
    idx = np.concatenate([np.random.permutation(S)[:H] for _ in range(K)])
    return {"x": x, "anchor": anchor, "offs": striped(idx)}


def reference(x, anchor, offs):
    idx = offs[:16].T.reshape(-1)
    a = f64(anchor).reshape(D, P, S)
    picked = np.stack([f64(x)[b][:, idx[b * S:(b + 1) * S]] for b in range(P)], axis=1)
    return np.concatenate([(picked * a).sum(axis=2), (picked * picked).sum(axis=2), (a * a).sum(axis=2)], axis=1)

@@ -1,0 +1,69 @@
+import concourse.mybir as mybir
+
+F32 = mybir.dt.float32
+U16 = mybir.dt.uint16
+MULT = mybir.AluOpType.mult
+COPY = mybir.ActivationFunctionType.Copy
+SQUARE = mybir.ActivationFunctionType.Square
+
+PARTS = 128
+PIECES = 4
+FEATURES = 512
+CHILDREN = 256
+BLOCKS = FEATURES // PARTS
+SUMS = 3 * PIECES
+OFFSET_COLUMNS = CHILDREN // 16
+
+
+def tile_ntxentlosschildrenfmapsclean_kernel(tc, x, anchor, offs, out):
+    nc = tc.nc
+
+    x_blocks = x.rearrange("b (p n) s -> b n p s", n=BLOCKS)
+    anchor_blocks = anchor.rearrange("(p n) j -> n p j", n=BLOCKS)
+    out_rows = out.rearrange("(p n) c -> p n c", n=BLOCKS)
+
+    with (
+        tc.tile_pool(name="held", bufs=1) as held,
+        tc.tile_pool(name="ring", bufs=4) as ring,
+    ):
+        offsets = held.tile([PARTS, PIECES * OFFSET_COLUMNS], U16, name="offsets")
+        nc.sync.dma_start(offsets[:], offs)
+
+        windows = {}
+        anchors = {}
+        for n in range(BLOCKS):
+            anchors[n] = held.tile([PARTS, PIECES * CHILDREN], F32, name=f"anchor{n}")
+            nc.scalar.dma_start(anchors[n][:], anchor_blocks[n])
+            for b in range(PIECES):
+                windows[n, b] = held.tile([PARTS, CHILDREN], F32, name=f"window{n}_{b}")
+                nc.sync.dma_start(windows[n, b][:], x_blocks[b, n])
+
+        sums = held.tile([PARTS, BLOCKS, SUMS], F32, name="sums")
+        anchor_norms = held.tile([PARTS, BLOCKS, PIECES], F32, name="anchor_norms")
+
+        for n in range(BLOCKS):
+            for b in range(PIECES):
+                piece = offsets[:, b * OFFSET_COLUMNS : (b + 1) * OFFSET_COLUMNS]
+                anchor_piece = anchors[n][:, b * CHILDREN : (b + 1) * CHILDREN]
+
+                picked = ring.tile([PARTS, CHILDREN], F32, name="picked")
+                nc.scalar.activation(picked[:], windows[n, b][:].indirect(piece), COPY)
+
+                product = ring.tile([PARTS, CHILDREN], F32, name="product")
+                nc.vector.scalar_tensor_tensor(
+                    product[:], picked[:], 1.0, anchor_piece, MULT, MULT,
+                    accum_out=sums[:, n, b : b + 1],
+                )
+                square = ring.tile([PARTS, CHILDREN], F32, name="square")
+                nc.vector.scalar_tensor_tensor(
+                    square[:], picked[:], 1.0, picked[:], MULT, MULT,
+                    accum_out=sums[:, n, PIECES + b : PIECES + b + 1],
+                )
+                anchor_square = ring.tile([PARTS, CHILDREN], F32, name="anchor_square")
+                nc.scalar.activation(
+                    anchor_square[:], anchor_piece, SQUARE,
+                    accum_out=anchor_norms[:, n, b : b + 1],
+                )
+
+        nc.vector.tensor_copy(sums[:, :, 2 * PIECES : SUMS], anchor_norms[:])
+        nc.sync.dma_start(out_rows, sums[:])

@@ -4,7 +4,6 @@ F32 = mybir.dt.float32
 U16 = mybir.dt.uint16
 MULT = mybir.AluOpType.mult
 COPY = mybir.ActivationFunctionType.Copy
-SQUARE = mybir.ActivationFunctionType.Square
 
 PARTS = 128
 PIECES = 4
@@ -19,7 +18,7 @@ def tile_ntxentlosschildrenfmapsclean_kernel(tc, x, anchor, offs, out):
     nc = tc.nc
 
     x_blocks = x.rearrange("b (p n) s -> b n p s", n=BLOCKS)
-    anchor_blocks = anchor.rearrange("(p n) j -> n p j", n=BLOCKS)
+    anchor_blocks = anchor.rearrange("(p n) (b s) -> n b p s", n=BLOCKS, s=CHILDREN)
     out_rows = out.rearrange("(p n) c -> p n c", n=BLOCKS)
 
     with (
@@ -32,38 +31,29 @@ def tile_ntxentlosschildrenfmapsclean_kernel(tc, x, anchor, offs, out):
         windows = {}
         anchors = {}
         for n in range(BLOCKS):
-            anchors[n] = held.tile([PARTS, PIECES * CHILDREN], F32, name=f"anchor{n}")
-            nc.scalar.dma_start(anchors[n][:], anchor_blocks[n])
             for b in range(PIECES):
+                anchors[n, b] = held.tile([PARTS, CHILDREN], F32, name=f"anchor{n}_{b}")
+                nc.sync.dma_start(anchors[n, b][:], anchor_blocks[n, b])
                 windows[n, b] = held.tile([PARTS, CHILDREN], F32, name=f"window{n}_{b}")
                 nc.sync.dma_start(windows[n, b][:], x_blocks[b, n])
 
         sums = held.tile([PARTS, BLOCKS, SUMS], F32, name="sums")
-        anchor_norms = held.tile([PARTS, BLOCKS, PIECES], F32, name="anchor_norms")
+
+        def sum_of_products(left, right, total):
+            products = ring.tile([PARTS, CHILDREN], F32, name="products")
+            nc.vector.scalar_tensor_tensor(
+                products[:], left, 1.0, right, MULT, MULT, accum_out=total
+            )
 
         for n in range(BLOCKS):
             for b in range(PIECES):
                 piece = offsets[:, b * OFFSET_COLUMNS : (b + 1) * OFFSET_COLUMNS]
-                anchor_piece = anchors[n][:, b * CHILDREN : (b + 1) * CHILDREN]
-
                 picked = ring.tile([PARTS, CHILDREN], F32, name="picked")
                 nc.scalar.activation(picked[:], windows[n, b][:].indirect(piece), COPY)
 
-                product = ring.tile([PARTS, CHILDREN], F32, name="product")
-                nc.vector.scalar_tensor_tensor(
-                    product[:], picked[:], 1.0, anchor_piece, MULT, MULT,
-                    accum_out=sums[:, n, b : b + 1],
-                )
-                square = ring.tile([PARTS, CHILDREN], F32, name="square")
-                nc.vector.scalar_tensor_tensor(
-                    square[:], picked[:], 1.0, picked[:], MULT, MULT,
-                    accum_out=sums[:, n, PIECES + b : PIECES + b + 1],
-                )
-                anchor_square = ring.tile([PARTS, CHILDREN], F32, name="anchor_square")
-                nc.scalar.activation(
-                    anchor_square[:], anchor_piece, SQUARE,
-                    accum_out=anchor_norms[:, n, b : b + 1],
-                )
+                anchor_piece = anchors[n, b][:]
+                sum_of_products(anchor_piece, anchor_piece, sums[:, n, 2 * PIECES + b : 2 * PIECES + b + 1])
+                sum_of_products(picked[:], anchor_piece, sums[:, n, b : b + 1])
+                sum_of_products(picked[:], picked[:], sums[:, n, PIECES + b : PIECES + b + 1])
 
-        nc.vector.tensor_copy(sums[:, :, 2 * PIECES : SUMS], anchor_norms[:])
         nc.sync.dma_start(out_rows, sums[:])

@@ -18,7 +18,7 @@ def tile_ntxentlosschildrenfmapsclean_kernel(tc, x, anchor, offs, out):
     nc = tc.nc
 
     x_blocks = x.rearrange("b (p n) s -> b n p s", n=BLOCKS)
-    anchor_blocks = anchor.rearrange("(p n) (b s) -> n b p s", n=BLOCKS, s=CHILDREN)
+    anchor_blocks = anchor.rearrange("(p n) j -> n p j", n=BLOCKS)
     out_rows = out.rearrange("(p n) c -> p n c", n=BLOCKS)
 
     with (
@@ -31,9 +31,9 @@ def tile_ntxentlosschildrenfmapsclean_kernel(tc, x, anchor, offs, out):
         windows = {}
         anchors = {}
         for n in range(BLOCKS):
+            anchors[n] = held.tile([PARTS, PIECES * CHILDREN], F32, name=f"anchor{n}")
+            nc.sync.dma_start(anchors[n][:], anchor_blocks[n])
             for b in range(PIECES):
-                anchors[n, b] = held.tile([PARTS, CHILDREN], F32, name=f"anchor{n}_{b}")
-                nc.sync.dma_start(anchors[n, b][:], anchor_blocks[n, b])
                 windows[n, b] = held.tile([PARTS, CHILDREN], F32, name=f"window{n}_{b}")
                 nc.sync.dma_start(windows[n, b][:], x_blocks[b, n])
 
@@ -51,7 +51,7 @@ def tile_ntxentlosschildrenfmapsclean_kernel(tc, x, anchor, offs, out):
                 picked = ring.tile([PARTS, CHILDREN], F32, name="picked")
                 nc.scalar.activation(picked[:], windows[n, b][:].indirect(piece), COPY)
 
-                anchor_piece = anchors[n, b][:]
+                anchor_piece = anchors[n][:, b * CHILDREN : (b + 1) * CHILDREN]
                 sum_of_products(anchor_piece, anchor_piece, sums[:, n, 2 * PIECES + b : 2 * PIECES + b + 1])
                 sum_of_products(picked[:], anchor_piece, sums[:, n, b : b + 1])
                 sum_of_products(picked[:], picked[:], sums[:, n, PIECES + b : PIECES + b + 1])

@@ -3,7 +3,9 @@ import concourse.mybir as mybir
 F32 = mybir.dt.float32
 U16 = mybir.dt.uint16
 MULT = mybir.AluOpType.mult
+ADD = mybir.AluOpType.add
 COPY = mybir.ActivationFunctionType.Copy
+SQUARE = mybir.ActivationFunctionType.Square
 
 PARTS = 128
 PIECES = 4
@@ -11,14 +13,21 @@ FEATURES = 512
 CHILDREN = 256
 BLOCKS = FEATURES // PARTS
 SUMS = 3 * PIECES
+NORMS = 2 * PIECES
 OFFSET_COLUMNS = CHILDREN // 16
+
+HALVES = 2
+FIELDS = 3
+MEAN = 1
+SPREAD = 2
+RECORD = 8
 
 
 def tile_ntxentlosschildrenfmapsclean_kernel(tc, x, anchor, offs, out):
     nc = tc.nc
 
     x_blocks = x.rearrange("b (p n) s -> b n p s", n=BLOCKS)
-    anchor_blocks = anchor.rearrange("(p n) j -> n p j", n=BLOCKS)
+    anchor_blocks = anchor.rearrange("(p n) (b s) -> n b p s", n=BLOCKS, s=CHILDREN)
     out_rows = out.rearrange("(p n) c -> p n c", n=BLOCKS)
 
     with (
@@ -31,19 +40,16 @@ def tile_ntxentlosschildrenfmapsclean_kernel(tc, x, anchor, offs, out):
         windows = {}
         anchors = {}
         for n in range(BLOCKS):
-            anchors[n] = held.tile([PARTS, PIECES * CHILDREN], F32, name=f"anchor{n}")
-            nc.sync.dma_start(anchors[n][:], anchor_blocks[n])
             for b in range(PIECES):
                 windows[n, b] = held.tile([PARTS, CHILDREN], F32, name=f"window{n}_{b}")
                 nc.sync.dma_start(windows[n, b][:], x_blocks[b, n])
+                anchors[n, b] = held.tile([PARTS, CHILDREN], F32, name=f"anchor{n}_{b}")
+                nc.sync.dma_start(anchors[n, b][:], anchor_blocks[n, b])
 
         sums = held.tile([PARTS, BLOCKS, SUMS], F32, name="sums")
 
-        def sum_of_products(left, right, total):
-            products = ring.tile([PARTS, CHILDREN], F32, name="products")
-            nc.vector.scalar_tensor_tensor(
-                products[:], left, 1.0, right, MULT, MULT, accum_out=total
-            )
+        stats = held.tile([PARTS, BLOCKS, NORMS, RECORD], F32, name="stats")
+        nc.scalar.memzero(stats[:])
 
         for n in range(BLOCKS):
             for b in range(PIECES):
@@ -51,9 +57,33 @@ def tile_ntxentlosschildrenfmapsclean_kernel(tc, x, anchor, offs, out):
                 picked = ring.tile([PARTS, CHILDREN], F32, name="picked")
                 nc.scalar.activation(picked[:], windows[n, b][:].indirect(piece), COPY)
 
-                anchor_piece = anchors[n][:, b * CHILDREN : (b + 1) * CHILDREN]
-                sum_of_products(anchor_piece, anchor_piece, sums[:, n, 2 * PIECES + b : 2 * PIECES + b + 1])
-                sum_of_products(picked[:], anchor_piece, sums[:, n, b : b + 1])
-                sum_of_products(picked[:], picked[:], sums[:, n, PIECES + b : PIECES + b + 1])
+                if b % 2 == 0:
+                    squares = ring.tile([PARTS, CHILDREN], F32, name="squares")
+                    nc.scalar.activation(
+                        squares[:], anchors[n, b][:], SQUARE,
+                        accum_out=stats[:, n, PIECES + b, SPREAD : SPREAD + 1],
+                    )
+                else:
+                    nc.vector.bn_stats(stats[:, n, PIECES + b, 0 : HALVES * FIELDS], anchors[n, b][:])
+
+                products = ring.tile([PARTS, CHILDREN], F32, name="products")
+                nc.vector.scalar_tensor_tensor(
+                    products[:], picked[:], 1.0, anchors[n, b][:], MULT, MULT,
+                    accum_out=sums[:, n, b : b + 1],
+                )
+                nc.vector.bn_stats(stats[:, n, b, 0 : HALVES * FIELDS], picked[:])
+
+        fields = stats[:, :, :, 0 : HALVES * FIELDS].rearrange("p n q (h f) -> p n q h f", f=FIELDS)
+        means = fields[:, :, :, :, MEAN]
+        spreads = fields[:, :, :, :, SPREAD]
+        mean_parts = held.tile([PARTS, BLOCKS, NORMS, HALVES], F32, name="mean_parts")
+        nc.vector.scalar_tensor_tensor(
+            mean_parts[:], means, float(CHILDREN // HALVES), means, MULT, MULT
+        )
+        half_norms = held.tile([PARTS, BLOCKS, NORMS, HALVES], F32, name="half_norms")
+        nc.vector.tensor_tensor(half_norms[:], mean_parts[:], spreads, ADD)
+        nc.vector.tensor_reduce(
+            sums[:, :, PIECES:SUMS], half_norms[:], axis=mybir.AxisListType.X, op=ADD
+        )
 
         nc.sync.dma_start(out_rows, sums[:])

@@ -3,7 +3,6 @@ import concourse.mybir as mybir
 F32 = mybir.dt.float32
 U16 = mybir.dt.uint16
 MULT = mybir.AluOpType.mult
-ADD = mybir.AluOpType.add
 COPY = mybir.ActivationFunctionType.Copy
 SQUARE = mybir.ActivationFunctionType.Square
 
@@ -13,14 +12,7 @@ FEATURES = 512
 CHILDREN = 256
 BLOCKS = FEATURES // PARTS
 SUMS = 3 * PIECES
-NORMS = 2 * PIECES
 OFFSET_COLUMNS = CHILDREN // 16
-
-HALVES = 2
-FIELDS = 3
-MEAN = 1
-SPREAD = 2
-RECORD = 8
 
 
 def tile_ntxentlosschildrenfmapsclean_kernel(tc, x, anchor, offs, out):
@@ -32,7 +24,7 @@ def tile_ntxentlosschildrenfmapsclean_kernel(tc, x, anchor, offs, out):
 
     with (
         tc.tile_pool(name="held", bufs=1) as held,
-        tc.tile_pool(name="ring", bufs=4) as ring,
+        tc.tile_pool(name="scratch", bufs=2) as scratch,
     ):
         offsets = held.tile([PARTS, PIECES * OFFSET_COLUMNS], U16, name="offsets")
         nc.sync.dma_start(offsets[:], offs)
@@ -47,43 +39,37 @@ def tile_ntxentlosschildrenfmapsclean_kernel(tc, x, anchor, offs, out):
                 nc.sync.dma_start(anchors[n, b][:], anchor_blocks[n, b])
 
         sums = held.tile([PARTS, BLOCKS, SUMS], F32, name="sums")
+        scalar_norms = held.tile([PARTS, BLOCKS - 1, PIECES], F32, name="scalar_norms")
 
-        stats = held.tile([PARTS, BLOCKS, NORMS, RECORD], F32, name="stats")
-        nc.scalar.memzero(stats[:])
+        nc.scalar.memzero(scalar_norms[:])
+
+        def sum_of_products(left, right, total):
+            products = scratch.tile([PARTS, CHILDREN], F32, name="products")
+            nc.vector.scalar_tensor_tensor(
+                products[:], left, 1.0, right, MULT, MULT, accum_out=total
+            )
 
         for n in range(BLOCKS):
             for b in range(PIECES):
                 piece = offsets[:, b * OFFSET_COLUMNS : (b + 1) * OFFSET_COLUMNS]
-                picked = ring.tile([PARTS, CHILDREN], F32, name="picked")
+                picked = held.tile([PARTS, CHILDREN], F32, name=f"picked{n}_{b}")
                 nc.scalar.activation(picked[:], windows[n, b][:].indirect(piece), COPY)
 
-                if b % 2 == 0:
-                    squares = ring.tile([PARTS, CHILDREN], F32, name="squares")
-                    nc.scalar.activation(
-                        squares[:], anchors[n, b][:], SQUARE,
-                        accum_out=stats[:, n, PIECES + b, SPREAD : SPREAD + 1],
+                if n == 0:
+                    sum_of_products(
+                        anchors[n, b][:], anchors[n, b][:],
+                        sums[:, n, 2 * PIECES + b : 2 * PIECES + b + 1],
                     )
-                else:
-                    nc.vector.bn_stats(stats[:, n, PIECES + b, 0 : HALVES * FIELDS], anchors[n, b][:])
+                sum_of_products(picked[:], anchors[n, b][:], sums[:, n, b : b + 1])
+                sum_of_products(picked[:], picked[:], sums[:, n, PIECES + b : PIECES + b + 1])
 
-                products = ring.tile([PARTS, CHILDREN], F32, name="products")
-                nc.vector.scalar_tensor_tensor(
-                    products[:], picked[:], 1.0, anchors[n, b][:], MULT, MULT,
-                    accum_out=sums[:, n, b : b + 1],
+        for n in range(1, BLOCKS):
+            for b in range(PIECES):
+                squares = scratch.tile([PARTS, CHILDREN], F32, name="squares")
+                nc.scalar.activation(
+                    squares[:], anchors[n, b][:], SQUARE,
+                    accum_out=scalar_norms[:, n - 1, b : b + 1],
                 )
-                nc.vector.bn_stats(stats[:, n, b, 0 : HALVES * FIELDS], picked[:])
 
-        fields = stats[:, :, :, 0 : HALVES * FIELDS].rearrange("p n q (h f) -> p n q h f", f=FIELDS)
-        means = fields[:, :, :, :, MEAN]
-        spreads = fields[:, :, :, :, SPREAD]
-        mean_parts = held.tile([PARTS, BLOCKS, NORMS, HALVES], F32, name="mean_parts")
-        nc.vector.scalar_tensor_tensor(
-            mean_parts[:], means, float(CHILDREN // HALVES), means, MULT, MULT
-        )
-        half_norms = held.tile([PARTS, BLOCKS, NORMS, HALVES], F32, name="half_norms")
-        nc.vector.tensor_tensor(half_norms[:], mean_parts[:], spreads, ADD)
-        nc.vector.tensor_reduce(
-            sums[:, :, PIECES:SUMS], half_norms[:], axis=mybir.AxisListType.X, op=ADD
-        )
-
+        nc.vector.tensor_copy(sums[:, 1:BLOCKS, 2 * PIECES : SUMS], scalar_norms[:])
         nc.sync.dma_start(out_rows, sums[:])

@@ -3,6 +3,7 @@ import concourse.mybir as mybir
 F32 = mybir.dt.float32
 U16 = mybir.dt.uint16
 MULT = mybir.AluOpType.mult
+ADD = mybir.AluOpType.add
 COPY = mybir.ActivationFunctionType.Copy
 SQUARE = mybir.ActivationFunctionType.Square
 
@@ -13,13 +14,17 @@ CHILDREN = 256
 BLOCKS = FEATURES // PARTS
 SUMS = 3 * PIECES
 OFFSET_COLUMNS = CHILDREN // 16
+PAIR = 2
+PAIRS = PIECES // PAIR
+STATS = 3
+VECTOR_NORMS = PIECES + PAIR
 
 
 def tile_ntxentlosschildrenfmapsclean_kernel(tc, x, anchor, offs, out):
     nc = tc.nc
 
     x_blocks = x.rearrange("b (p n) s -> b n p s", n=BLOCKS)
-    anchor_blocks = anchor.rearrange("(p n) (b s) -> n b p s", n=BLOCKS, s=CHILDREN)
+    anchor_blocks = anchor.rearrange("(p n) (h s) -> n h p s", n=BLOCKS, s=PAIR * CHILDREN)
     out_rows = out.rearrange("(p n) c -> p n c", n=BLOCKS)
 
     with (
@@ -32,44 +37,54 @@ def tile_ntxentlosschildrenfmapsclean_kernel(tc, x, anchor, offs, out):
         windows = {}
         anchors = {}
         for n in range(BLOCKS):
-            for b in range(PIECES):
-                windows[n, b] = held.tile([PARTS, CHILDREN], F32, name=f"window{n}_{b}")
-                nc.sync.dma_start(windows[n, b][:], x_blocks[b, n])
-                anchors[n, b] = held.tile([PARTS, CHILDREN], F32, name=f"anchor{n}_{b}")
-                nc.sync.dma_start(anchors[n, b][:], anchor_blocks[n, b])
+            for h in range(PAIRS):
+                for b in range(h * PAIR, (h + 1) * PAIR):
+                    windows[n, b] = held.tile([PARTS, CHILDREN], F32, name=f"window{n}_{b}")
+                    nc.sync.dma_start(windows[n, b][:], x_blocks[b, n])
+                anchors[n, h] = held.tile([PARTS, PAIR * CHILDREN], F32, name=f"anchor{n}_{h}")
+                nc.sync.dma_start(anchors[n, h][:], anchor_blocks[n, h])
 
         sums = held.tile([PARTS, BLOCKS, SUMS], F32, name="sums")
-        scalar_norms = held.tile([PARTS, BLOCKS - 1, PIECES], F32, name="scalar_norms")
+        stats = held.tile([PARTS, BLOCKS, VECTOR_NORMS, STATS], F32, name="stats")
 
-        nc.scalar.memzero(scalar_norms[:])
+        warm = held.tile([PARTS, 1], F32, name="warm")
+        nc.scalar.memzero(warm[:])
 
-        def sum_of_products(left, right, total):
-            products = scratch.tile([PARTS, CHILDREN], F32, name="products")
-            nc.vector.scalar_tensor_tensor(
-                products[:], left, 1.0, right, MULT, MULT, accum_out=total
+        def stats_of_pair(pair, n, first):
+            nc.vector.bn_stats(
+                stats[:, n, first : first + PAIR, :],
+                pair.rearrange("p (two s) -> p s two", two=PAIR),
             )
 
         for n in range(BLOCKS):
-            for b in range(PIECES):
-                piece = offsets[:, b * OFFSET_COLUMNS : (b + 1) * OFFSET_COLUMNS]
-                picked = held.tile([PARTS, CHILDREN], F32, name=f"picked{n}_{b}")
-                nc.scalar.activation(picked[:], windows[n, b][:].indirect(piece), COPY)
-
-                if n == 0:
-                    sum_of_products(
-                        anchors[n, b][:], anchors[n, b][:],
-                        sums[:, n, 2 * PIECES + b : 2 * PIECES + b + 1],
+            for h in range(PAIRS):
+                picked = held.tile([PARTS, PAIR * CHILDREN], F32, name=f"picked{n}_{h}")
+                for b in range(h * PAIR, (h + 1) * PAIR):
+                    columns = slice((b - h * PAIR) * CHILDREN, (b - h * PAIR + 1) * CHILDREN)
+                    piece = offsets[:, b * OFFSET_COLUMNS : (b + 1) * OFFSET_COLUMNS]
+                    nc.scalar.activation(
+                        picked[:, columns], windows[n, b][:].indirect(piece), COPY
                     )
-                sum_of_products(picked[:], anchors[n, b][:], sums[:, n, b : b + 1])
-                sum_of_products(picked[:], picked[:], sums[:, n, PIECES + b : PIECES + b + 1])
+                    products = scratch.tile([PARTS, CHILDREN], F32, name="products")
+                    nc.vector.scalar_tensor_tensor(
+                        products[:], picked[:, columns], 1.0, anchors[n, h][:, columns],
+                        MULT, MULT, accum_out=sums[:, n, b : b + 1],
+                    )
+                stats_of_pair(picked[:], n, h * PAIR)
 
-        for n in range(1, BLOCKS):
-            for b in range(PIECES):
+            stats_of_pair(anchors[n, 0][:], n, PIECES)
+            for b in range(PAIR, PIECES):
+                columns = slice((b - PAIR) * CHILDREN, (b - PAIR + 1) * CHILDREN)
                 squares = scratch.tile([PARTS, CHILDREN], F32, name="squares")
                 nc.scalar.activation(
-                    squares[:], anchors[n, b][:], SQUARE,
-                    accum_out=scalar_norms[:, n - 1, b : b + 1],
+                    squares[:], anchors[n, 1][:, columns], SQUARE,
+                    accum_out=sums[:, n, 2 * PIECES + b : 2 * PIECES + b + 1],
                 )
 
-        nc.vector.tensor_copy(sums[:, 1:BLOCKS, 2 * PIECES : SUMS], scalar_norms[:])
+        mean_squares = held.tile([PARTS, BLOCKS, VECTOR_NORMS], F32, name="mean_squares")
+        nc.vector.tensor_tensor(mean_squares[:], stats[:, :, :, 1], stats[:, :, :, 1], MULT)
+        nc.vector.scalar_tensor_tensor(
+            sums[:, :, PIECES : PIECES + VECTOR_NORMS], mean_squares[:], float(CHILDREN),
+            stats[:, :, :, 2], MULT, ADD,
+        )
         nc.sync.dma_start(out_rows, sums[:])

@@ -6,6 +6,7 @@ MULT = mybir.AluOpType.mult
 ADD = mybir.AluOpType.add
 COPY = mybir.ActivationFunctionType.Copy
 SQUARE = mybir.ActivationFunctionType.Square
+INNERMOST = mybir.AxisListType.X
 
 PARTS = 128
 PIECES = 4
@@ -17,7 +18,7 @@ OFFSET_COLUMNS = CHILDREN // 16
 PAIR = 2
 PAIRS = PIECES // PAIR
 STATS = 3
-VECTOR_NORMS = PIECES + PAIR
+NORMS = 2 * PIECES
 
 
 def tile_ntxentlosschildrenfmapsclean_kernel(tc, x, anchor, offs, out):
@@ -45,7 +46,7 @@ def tile_ntxentlosschildrenfmapsclean_kernel(tc, x, anchor, offs, out):
                 nc.sync.dma_start(anchors[n, h][:], anchor_blocks[n, h])
 
         sums = held.tile([PARTS, BLOCKS, SUMS], F32, name="sums")
-        stats = held.tile([PARTS, BLOCKS, VECTOR_NORMS, STATS], F32, name="stats")
+        stats = held.tile([PARTS, BLOCKS, NORMS, STATS], F32, name="stats")
 
         warm = held.tile([PARTS, 1], F32, name="warm")
         nc.scalar.memzero(warm[:])
@@ -56,6 +57,15 @@ def tile_ntxentlosschildrenfmapsclean_kernel(tc, x, anchor, offs, out):
                 pair.rearrange("p (two s) -> p s two", two=PAIR),
             )
 
+        def sums_of_products(products, n, h):
+            nc.vector.tensor_reduce(
+                sums[:, n, h * PAIR : (h + 1) * PAIR],
+                products.rearrange("p (two s) -> p two s", two=PAIR),
+                INNERMOST, ADD,
+            )
+
+        waiting = None
+        last = (BLOCKS - 1, PAIRS - 1)
         for n in range(BLOCKS):
             for h in range(PAIRS):
                 picked = held.tile([PARTS, PAIR * CHILDREN], F32, name=f"picked{n}_{h}")
@@ -65,26 +75,46 @@ def tile_ntxentlosschildrenfmapsclean_kernel(tc, x, anchor, offs, out):
                     nc.scalar.activation(
                         picked[:, columns], windows[n, b][:].indirect(piece), COPY
                     )
-                    products = scratch.tile([PARTS, CHILDREN], F32, name="products")
-                    nc.vector.scalar_tensor_tensor(
-                        products[:], picked[:, columns], 1.0, anchors[n, h][:, columns],
-                        MULT, MULT, accum_out=sums[:, n, b : b + 1],
-                    )
+                if n < BLOCKS - 1:
+                    stats_of_pair(anchors[n, h][:], n, PIECES + h * PAIR)
+                previous = waiting
+                if (n, h) != last:
+                    products = held.tile([PARTS, PAIR * CHILDREN], F32, name=f"products{n}_{h}")
+                    nc.gpsimd.tensor_tensor(products[:], picked[:], anchors[n, h][:], MULT)
+                    waiting = (products[:], n, h)
                 stats_of_pair(picked[:], n, h * PAIR)
+                if previous is not None:
+                    sums_of_products(*previous)
 
-            stats_of_pair(anchors[n, 0][:], n, PIECES)
-            for b in range(PAIR, PIECES):
-                columns = slice((b - PAIR) * CHILDREN, (b - PAIR + 1) * CHILDREN)
-                squares = scratch.tile([PARTS, CHILDREN], F32, name="squares")
-                nc.scalar.activation(
-                    squares[:], anchors[n, 1][:, columns], SQUARE,
-                    accum_out=sums[:, n, 2 * PIECES + b : 2 * PIECES + b + 1],
-                )
+        n, h = last
+        for b in range(h * PAIR, (h + 1) * PAIR):
+            columns = slice((b - h * PAIR) * CHILDREN, (b - h * PAIR + 1) * CHILDREN)
+            unkept = scratch.tile([PARTS, CHILDREN], F32, name="unkept")
+            nc.vector.scalar_tensor_tensor(
+                unkept[:], picked[:, columns], 1.0, anchors[n, h][:, columns],
+                MULT, MULT, accum_out=sums[:, n, b : b + 1],
+            )
 
-        mean_squares = held.tile([PARTS, BLOCKS, VECTOR_NORMS], F32, name="mean_squares")
-        nc.vector.tensor_tensor(mean_squares[:], stats[:, :, :, 1], stats[:, :, :, 1], MULT)
-        nc.vector.scalar_tensor_tensor(
-            sums[:, :, PIECES : PIECES + VECTOR_NORMS], mean_squares[:], float(CHILDREN),
-            stats[:, :, :, 2], MULT, ADD,
-        )
+        for b in range(PIECES):
+            columns = slice((b % PAIR) * CHILDREN, (b % PAIR + 1) * CHILDREN)
+            squares = scratch.tile([PARTS, CHILDREN], F32, name="squares")
+            nc.scalar.activation(
+                squares[:], anchors[n, b // PAIR][:, columns], SQUARE,
+                accum_out=sums[:, n, 2 * PIECES + b : 2 * PIECES + b + 1],
+            )
+
+        mean_squares = held.tile([PARTS, BLOCKS, NORMS], F32, name="mean_squares")
+        for blocks, norms in (
+            (slice(0, BLOCKS - 1), slice(0, NORMS)),
+            (slice(BLOCKS - 1, BLOCKS), slice(0, PIECES)),
+        ):
+            nc.vector.tensor_tensor(
+                mean_squares[:, blocks, norms],
+                stats[:, blocks, norms, 1], stats[:, blocks, norms, 1], MULT,
+            )
+            nc.vector.scalar_tensor_tensor(
+                sums[:, blocks, PIECES + norms.start : PIECES + norms.stop],
+                mean_squares[:, blocks, norms], float(CHILDREN),
+                stats[:, blocks, norms, 2], MULT, ADD,
+            )
         nc.sync.dma_start(out_rows, sums[:])

@@ -13,6 +13,7 @@ PIECES = 4
 FEATURES = 512
 CHILDREN = 256
 BLOCKS = FEATURES // PARTS
+LAST = BLOCKS - 1
 SUMS = 3 * PIECES
 OFFSET_COLUMNS = CHILDREN // 16
 PAIR = 2
@@ -46,10 +47,13 @@ def tile_ntxentlosschildrenfmapsclean_kernel(tc, x, anchor, offs, out):
                 nc.sync.dma_start(anchors[n, h][:], anchor_blocks[n, h])
 
         sums = held.tile([PARTS, BLOCKS, SUMS], F32, name="sums")
-        stats = held.tile([PARTS, BLOCKS, NORMS, STATS], F32, name="stats")
+        stats = held.tile([PARTS, LAST, NORMS, STATS], F32, name="stats")
 
         warm = held.tile([PARTS, 1], F32, name="warm")
         nc.scalar.memzero(warm[:])
+
+        def columns_of(b):
+            return slice((b % PAIR) * CHILDREN, (b % PAIR + 1) * CHILDREN)
 
         def stats_of_pair(pair, n, first):
             nc.vector.bn_stats(
@@ -64,57 +68,48 @@ def tile_ntxentlosschildrenfmapsclean_kernel(tc, x, anchor, offs, out):
                 INNERMOST, ADD,
             )
 
+        picked = {}
         waiting = None
-        last = (BLOCKS - 1, PAIRS - 1)
         for n in range(BLOCKS):
             for h in range(PAIRS):
-                picked = held.tile([PARTS, PAIR * CHILDREN], F32, name=f"picked{n}_{h}")
+                picked[n, h] = held.tile([PARTS, PAIR * CHILDREN], F32, name=f"picked{n}_{h}")
                 for b in range(h * PAIR, (h + 1) * PAIR):
-                    columns = slice((b - h * PAIR) * CHILDREN, (b - h * PAIR + 1) * CHILDREN)
                     piece = offsets[:, b * OFFSET_COLUMNS : (b + 1) * OFFSET_COLUMNS]
                     nc.scalar.activation(
-                        picked[:, columns], windows[n, b][:].indirect(piece), COPY
+                        picked[n, h][:, columns_of(b)], windows[n, b][:].indirect(piece), COPY
                     )
-                if n < BLOCKS - 1:
+                if n < LAST:
                     stats_of_pair(anchors[n, h][:], n, PIECES + h * PAIR)
                 previous = waiting
-                if (n, h) != last:
+                if (n, h) != (LAST, PAIRS - 1):
                     products = held.tile([PARTS, PAIR * CHILDREN], F32, name=f"products{n}_{h}")
-                    nc.gpsimd.tensor_tensor(products[:], picked[:], anchors[n, h][:], MULT)
+                    nc.gpsimd.tensor_tensor(products[:], picked[n, h][:], anchors[n, h][:], MULT)
                     waiting = (products[:], n, h)
-                stats_of_pair(picked[:], n, h * PAIR)
+                if n < LAST:
+                    stats_of_pair(picked[n, h][:], n, h * PAIR)
                 if previous is not None:
                     sums_of_products(*previous)
 
-        n, h = last
-        for b in range(h * PAIR, (h + 1) * PAIR):
-            columns = slice((b - h * PAIR) * CHILDREN, (b - h * PAIR + 1) * CHILDREN)
+        for b in range(PIECES - PAIR, PIECES):
             unkept = scratch.tile([PARTS, CHILDREN], F32, name="unkept")
             nc.vector.scalar_tensor_tensor(
-                unkept[:], picked[:, columns], 1.0, anchors[n, h][:, columns],
-                MULT, MULT, accum_out=sums[:, n, b : b + 1],
+                unkept[:], picked[LAST, PAIRS - 1][:, columns_of(b)], 1.0,
+                anchors[LAST, PAIRS - 1][:, columns_of(b)],
+                MULT, MULT, accum_out=sums[:, LAST, b : b + 1],
             )
 
-        for b in range(PIECES):
-            columns = slice((b % PAIR) * CHILDREN, (b % PAIR + 1) * CHILDREN)
-            squares = scratch.tile([PARTS, CHILDREN], F32, name="squares")
-            nc.scalar.activation(
-                squares[:], anchors[n, b // PAIR][:, columns], SQUARE,
-                accum_out=sums[:, n, 2 * PIECES + b : 2 * PIECES + b + 1],
-            )
+        for first, tiles in ((2 * PIECES, anchors), (PIECES, picked)):
+            for b in range(PIECES):
+                squares = scratch.tile([PARTS, CHILDREN], F32, name="squares")
+                nc.scalar.activation(
+                    squares[:], tiles[LAST, b // PAIR][:, columns_of(b)], SQUARE,
+                    accum_out=sums[:, LAST, first + b : first + b + 1],
+                )
 
-        mean_squares = held.tile([PARTS, BLOCKS, NORMS], F32, name="mean_squares")
-        for blocks, norms in (
-            (slice(0, BLOCKS - 1), slice(0, NORMS)),
-            (slice(BLOCKS - 1, BLOCKS), slice(0, PIECES)),
-        ):
-            nc.vector.tensor_tensor(
-                mean_squares[:, blocks, norms],
-                stats[:, blocks, norms, 1], stats[:, blocks, norms, 1], MULT,
-            )
-            nc.vector.scalar_tensor_tensor(
-                sums[:, blocks, PIECES + norms.start : PIECES + norms.stop],
-                mean_squares[:, blocks, norms], float(CHILDREN),
-                stats[:, blocks, norms, 2], MULT, ADD,
-            )
+        mean_squares = held.tile([PARTS, LAST, NORMS], F32, name="mean_squares")
+        nc.vector.tensor_tensor(mean_squares[:], stats[:, :, :, 1], stats[:, :, :, 1], MULT)
+        nc.vector.scalar_tensor_tensor(
+            sums[:, 0:LAST, PIECES:SUMS], mean_squares[:], float(CHILDREN),
+            stats[:, :, :, 2], MULT, ADD,
+        )
         nc.sync.dma_start(out_rows, sums[:])

@@ -43,8 +43,11 @@ def tile_ntxentlosschildrenfmapsclean_kernel(tc, x, anchor, offs, out):
                 for b in range(h * PAIR, (h + 1) * PAIR):
                     windows[n, b] = held.tile([PARTS, CHILDREN], F32, name=f"window{n}_{b}")
                     nc.sync.dma_start(windows[n, b][:], x_blocks[b, n])
-                anchors[n, h] = held.tile([PARTS, PAIR * CHILDREN], F32, name=f"anchor{n}_{h}")
-                nc.sync.dma_start(anchors[n, h][:], anchor_blocks[n, h])
+                    if b % PAIR == 0:
+                        anchors[n, h] = held.tile(
+                            [PARTS, PAIR * CHILDREN], F32, name=f"anchor{n}_{h}"
+                        )
+                        nc.sync.dma_start(anchors[n, h][:], anchor_blocks[n, h])
 
         sums = held.tile([PARTS, BLOCKS, SUMS], F32, name="sums")
         stats = held.tile([PARTS, LAST, NORMS, STATS], F32, name="stats")

@@ -1,4 +1,5 @@
 import concourse.mybir as mybir
+from concourse.masks import make_identity
 
 F32 = mybir.dt.float32
 U16 = mybir.dt.uint16
@@ -20,6 +21,10 @@ PAIR = 2
 PAIRS = PIECES // PAIR
 STATS = 3
 NORMS = 2 * PIECES
+BANK = 512
+CHUNKS = 4
+WIDTH = CHILDREN // CHUNKS
+FOLDED = BANK // (PIECES * WIDTH)
 
 
 def tile_ntxentlosschildrenfmapsclean_kernel(tc, x, anchor, offs, out):
@@ -32,6 +37,7 @@ def tile_ntxentlosschildrenfmapsclean_kernel(tc, x, anchor, offs, out):
     with (
         tc.tile_pool(name="held", bufs=1) as held,
         tc.tile_pool(name="scratch", bufs=2) as scratch,
+        tc.psum_pool(name="banks", bufs=1) as banks,
     ):
         offsets = held.tile([PARTS, PIECES * OFFSET_COLUMNS], U16, name="offsets")
         nc.sync.dma_start(offsets[:], offs)
@@ -48,6 +54,9 @@ def tile_ntxentlosschildrenfmapsclean_kernel(tc, x, anchor, offs, out):
                             [PARTS, PAIR * CHILDREN], F32, name=f"anchor{n}_{h}"
                         )
                         nc.sync.dma_start(anchors[n, h][:], anchor_blocks[n, h])
+
+        identity = held.tile([PARTS, PARTS], F32, name="identity")
+        make_identity(nc, identity[:])
 
         sums = held.tile([PARTS, BLOCKS, SUMS], F32, name="sums")
         stats = held.tile([PARTS, LAST, NORMS, STATS], F32, name="stats")
@@ -72,6 +81,7 @@ def tile_ntxentlosschildrenfmapsclean_kernel(tc, x, anchor, offs, out):
             )
 
         picked = {}
+        folded = banks.tile([PARTS, FOLDED, PIECES, WIDTH], F32, name="folded")
         waiting = None
         for n in range(BLOCKS):
             for h in range(PAIRS):
@@ -83,11 +93,22 @@ def tile_ntxentlosschildrenfmapsclean_kernel(tc, x, anchor, offs, out):
                     )
                 if n < LAST:
                     stats_of_pair(anchors[n, h][:], n, PIECES + h * PAIR)
-                previous = waiting
+                previous, waiting = waiting, None
                 if (n, h) != (LAST, PAIRS - 1):
                     products = held.tile([PARTS, PAIR * CHILDREN], F32, name=f"products{n}_{h}")
                     nc.gpsimd.tensor_tensor(products[:], picked[n, h][:], anchors[n, h][:], MULT)
-                    waiting = (products[:], n, h)
+                    if n < FOLDED:
+                        chunked = products[:].rearrange(
+                            "p (two c w) -> p two c w", two=PAIR, c=CHUNKS
+                        )
+                        for c in range(CHUNKS):
+                            nc.tensor.matmul(
+                                folded[:, n, h * PAIR : (h + 1) * PAIR, :],
+                                identity[:], chunked[:, :, c, :],
+                                start=(c == 0), stop=(c == CHUNKS - 1),
+                            )
+                    else:
+                        waiting = (products[:], n, h)
                 if n < LAST:
                     stats_of_pair(picked[n, h][:], n, h * PAIR)
                 if previous is not None:
@@ -115,4 +136,5 @@ def tile_ntxentlosschildrenfmapsclean_kernel(tc, x, anchor, offs, out):
             sums[:, 0:LAST, PIECES:SUMS], mean_squares[:], float(CHILDREN),
             stats[:, :, :, 2], MULT, ADD,
         )
+        nc.vector.tensor_reduce(sums[:, 0:FOLDED, 0:PIECES], folded[:], INNERMOST, ADD)
         nc.sync.dma_start(out_rows, sums[:])

@@ -44,16 +44,25 @@ def tile_ntxentlosschildrenfmapsclean_kernel(tc, x, anchor, offs, out):
 
         windows = {}
         anchors = {}
-        for n in range(BLOCKS):
-            for h in range(PAIRS):
-                for b in range(h * PAIR, (h + 1) * PAIR):
-                    windows[n, b] = held.tile([PARTS, CHILDREN], F32, name=f"window{n}_{b}")
-                    nc.sync.dma_start(windows[n, b][:], x_blocks[b, n])
-                    if b % PAIR == 0:
-                        anchors[n, h] = held.tile(
-                            [PARTS, PAIR * CHILDREN], F32, name=f"anchor{n}_{h}"
-                        )
-                        nc.sync.dma_start(anchors[n, h][:], anchor_blocks[n, h])
+
+        def load_windows(n, h):
+            for b in range(h * PAIR, (h + 1) * PAIR):
+                windows[n, b] = held.tile([PARTS, CHILDREN], F32, name=f"window{n}_{b}")
+                nc.sync.dma_start(windows[n, b][:], x_blocks[b, n])
+                if (n, b) == (0, 0):
+                    load_anchors(n, h)
+
+        def load_anchors(n, h):
+            anchors[n, h] = held.tile([PARTS, PAIR * CHILDREN], F32, name=f"anchor{n}_{h}")
+            nc.sync.dma_start(anchors[n, h][:], anchor_blocks[n, h])
+
+        pairs = [(n, h) for n in range(BLOCKS) for h in range(PAIRS)]
+        load_windows(*pairs[0])
+        load_windows(*pairs[1])
+        for before, after in zip(pairs[1:], pairs[2:]):
+            load_anchors(*before)
+            load_windows(*after)
+        load_anchors(*pairs[-1])
 
         identity = held.tile([PARTS, PARTS], F32, name="identity")
         make_identity(nc, identity[:])

@@ -15,12 +15,13 @@ FEATURES = 512
 CHILDREN = 256
 BLOCKS = FEATURES // PARTS
 LAST = BLOCKS - 1
-SUMS = 3 * PIECES
 OFFSET_COLUMNS = CHILDREN // 16
 PAIR = 2
 PAIRS = PIECES // PAIR
+DOT, PICKED, ANCHOR = 0, 1, 2
+KINDS = 3
+NORMS = (PICKED, ANCHOR)
 STATS = 3
-NORMS = 2 * PIECES
 BANK = 512
 CHUNKS = 4
 WIDTH = CHILDREN // CHUNKS
@@ -42,33 +43,29 @@ def tile_ntxentlosschildrenfmapsclean_kernel(tc, x, anchor, offs, out):
         offsets = held.tile([PARTS, PIECES * OFFSET_COLUMNS], U16, name="offsets")
         nc.sync.dma_start(offsets[:], offs)
 
+        pairs = [(n, h) for n in range(BLOCKS) for h in range(PAIRS)]
         windows = {}
         anchors = {}
-
-        def load_windows(n, h):
-            for b in range(h * PAIR, (h + 1) * PAIR):
-                windows[n, b] = held.tile([PARTS, CHILDREN], F32, name=f"window{n}_{b}")
-                nc.sync.dma_start(windows[n, b][:], x_blocks[b, n])
-                if (n, b) == (0, 0):
-                    load_anchors(n, h)
 
         def load_anchors(n, h):
             anchors[n, h] = held.tile([PARTS, PAIR * CHILDREN], F32, name=f"anchor{n}_{h}")
             nc.sync.dma_start(anchors[n, h][:], anchor_blocks[n, h])
 
-        pairs = [(n, h) for n in range(BLOCKS) for h in range(PAIRS)]
-        load_windows(*pairs[0])
-        load_windows(*pairs[1])
-        for before, after in zip(pairs[1:], pairs[2:]):
-            load_anchors(*before)
-            load_windows(*after)
-        load_anchors(*pairs[-1])
+        for n, h in pairs:
+            if n == LAST:
+                load_anchors(n, h)
+            for b in range(h * PAIR, (h + 1) * PAIR):
+                windows[n, b] = held.tile([PARTS, CHILDREN], F32, name=f"window{n}_{b}")
+                nc.sync.dma_start(windows[n, b][:], x_blocks[b, n])
+            if n < LAST:
+                load_anchors(n, h)
 
         identity = held.tile([PARTS, PARTS], F32, name="identity")
         make_identity(nc, identity[:])
 
-        sums = held.tile([PARTS, BLOCKS, SUMS], F32, name="sums")
-        stats = held.tile([PARTS, LAST, NORMS, STATS], F32, name="stats")
+        sums = held.tile([PARTS, BLOCKS, KINDS, PIECES], F32, name="sums")
+        stats = held.tile([PARTS, BLOCKS, len(NORMS), PIECES, STATS], F32, name="stats")
+        mean_squares = held.tile([PARTS, BLOCKS, len(NORMS), PIECES], F32, name="mean_squares")
 
         warm = held.tile([PARTS, 1], F32, name="warm")
         nc.scalar.memzero(warm[:])
@@ -76,74 +73,86 @@ def tile_ntxentlosschildrenfmapsclean_kernel(tc, x, anchor, offs, out):
         def columns_of(b):
             return slice((b % PAIR) * CHILDREN, (b % PAIR + 1) * CHILDREN)
 
-        def stats_of_pair(pair, n, first):
+        def stats_of_pair(tiles, kind, n, h):
             nc.vector.bn_stats(
-                stats[:, n, first : first + PAIR, :],
-                pair.rearrange("p (two s) -> p s two", two=PAIR),
+                stats[:, n, NORMS.index(kind), h * PAIR : (h + 1) * PAIR, :],
+                tiles[n, h][:].rearrange("p (two s) -> p s two", two=PAIR),
             )
 
-        def sums_of_products(products, n, h):
+        def norms_from_stats(blocks, kinds, pieces):
+            rows = slice(NORMS.index(kinds.start), NORMS.index(kinds.stop - 1) + 1)
+            squares = mean_squares[:, blocks, rows, pieces]
+            nc.vector.tensor_tensor(
+                squares, stats[:, blocks, rows, pieces, 1], stats[:, blocks, rows, pieces, 1], MULT
+            )
+            nc.vector.scalar_tensor_tensor(
+                sums[:, blocks, kinds, pieces], squares, float(CHILDREN),
+                stats[:, blocks, rows, pieces, 2], MULT, ADD,
+            )
+
+        def sums_of_products(n, h):
             nc.vector.tensor_reduce(
-                sums[:, n, h * PAIR : (h + 1) * PAIR],
-                products.rearrange("p (two s) -> p two s", two=PAIR),
+                sums[:, n, DOT, h * PAIR : (h + 1) * PAIR],
+                products[n, h][:].rearrange("p (two s) -> p two s", two=PAIR),
                 INNERMOST, ADD,
             )
 
         picked = {}
+        products = {}
         folded = banks.tile([PARTS, FOLDED, PIECES, WIDTH], F32, name="folded")
+        folded_late = banks.tile([PARTS, PAIR, WIDTH], F32, name="folded_late")
         waiting = None
-        for n in range(BLOCKS):
-            for h in range(PAIRS):
-                picked[n, h] = held.tile([PARTS, PAIR * CHILDREN], F32, name=f"picked{n}_{h}")
-                for b in range(h * PAIR, (h + 1) * PAIR):
-                    piece = offsets[:, b * OFFSET_COLUMNS : (b + 1) * OFFSET_COLUMNS]
-                    nc.scalar.activation(
-                        picked[n, h][:, columns_of(b)], windows[n, b][:].indirect(piece), COPY
+        for n, h in pairs:
+            picked[n, h] = held.tile([PARTS, PAIR * CHILDREN], F32, name=f"picked{n}_{h}")
+            for b in range(h * PAIR, (h + 1) * PAIR):
+                piece = offsets[:, b * OFFSET_COLUMNS : (b + 1) * OFFSET_COLUMNS]
+                nc.scalar.activation(
+                    picked[n, h][:, columns_of(b)], windows[n, b][:].indirect(piece), COPY
+                )
+            if n < LAST or h == 0:
+                stats_of_pair(anchors, ANCHOR, n, h)
+            previous, waiting = waiting, None
+            if (n, h) != pairs[-1]:
+                products[n, h] = held.tile([PARTS, PAIR * CHILDREN], F32, name=f"products{n}_{h}")
+                nc.gpsimd.tensor_tensor(products[n, h][:], picked[n, h][:], anchors[n, h][:], MULT)
+                if n < FOLDED or (n, h) == (FOLDED, 0):
+                    chunked = products[n, h][:].rearrange(
+                        "p (two c w) -> p two c w", two=PAIR, c=CHUNKS
                     )
-                if n < LAST:
-                    stats_of_pair(anchors[n, h][:], n, PIECES + h * PAIR)
-                previous, waiting = waiting, None
-                if (n, h) != (LAST, PAIRS - 1):
-                    products = held.tile([PARTS, PAIR * CHILDREN], F32, name=f"products{n}_{h}")
-                    nc.gpsimd.tensor_tensor(products[:], picked[n, h][:], anchors[n, h][:], MULT)
                     if n < FOLDED:
-                        chunked = products[:].rearrange(
-                            "p (two c w) -> p two c w", two=PAIR, c=CHUNKS
-                        )
-                        for c in range(CHUNKS):
-                            nc.tensor.matmul(
-                                folded[:, n, h * PAIR : (h + 1) * PAIR, :],
-                                identity[:], chunked[:, :, c, :],
-                                start=(c == 0), stop=(c == CHUNKS - 1),
-                            )
+                        target = folded[:, n, h * PAIR : (h + 1) * PAIR, :]
                     else:
-                        waiting = (products[:], n, h)
-                if n < LAST:
-                    stats_of_pair(picked[n, h][:], n, h * PAIR)
-                if previous is not None:
-                    sums_of_products(*previous)
+                        target = folded_late[:]
+                    for c in range(CHUNKS):
+                        nc.tensor.matmul(
+                            target, identity[:], chunked[:, :, c, :],
+                            start=(c == 0), stop=(c == CHUNKS - 1),
+                        )
+                else:
+                    waiting = (n, h)
+            if n < LAST:
+                stats_of_pair(picked, PICKED, n, h)
+            if previous is not None:
+                sums_of_products(*previous)
 
         for b in range(PIECES - PAIR, PIECES):
             unkept = scratch.tile([PARTS, CHILDREN], F32, name="unkept")
             nc.vector.scalar_tensor_tensor(
-                unkept[:], picked[LAST, PAIRS - 1][:, columns_of(b)], 1.0,
-                anchors[LAST, PAIRS - 1][:, columns_of(b)],
-                MULT, MULT, accum_out=sums[:, LAST, b : b + 1],
+                unkept[:], picked[pairs[-1]][:, columns_of(b)], 1.0,
+                anchors[pairs[-1]][:, columns_of(b)],
+                MULT, MULT, accum_out=sums[:, LAST, DOT, b : b + 1],
             )
 
-        for first, tiles in ((2 * PIECES, anchors), (PIECES, picked)):
-            for b in range(PIECES):
+        for kind, tiles, first in ((ANCHOR, anchors, PAIR), (PICKED, picked, 0)):
+            for b in range(first, PIECES):
                 squares = scratch.tile([PARTS, CHILDREN], F32, name="squares")
                 nc.scalar.activation(
                     squares[:], tiles[LAST, b // PAIR][:, columns_of(b)], SQUARE,
-                    accum_out=sums[:, LAST, first + b : first + b + 1],
+                    accum_out=sums[:, LAST, kind, b : b + 1],
                 )
 
-        mean_squares = held.tile([PARTS, LAST, NORMS], F32, name="mean_squares")
-        nc.vector.tensor_tensor(mean_squares[:], stats[:, :, :, 1], stats[:, :, :, 1], MULT)
-        nc.vector.scalar_tensor_tensor(
-            sums[:, 0:LAST, PIECES:SUMS], mean_squares[:], float(CHILDREN),
-            stats[:, :, :, 2], MULT, ADD,
-        )
-        nc.vector.tensor_reduce(sums[:, 0:FOLDED, 0:PIECES], folded[:], INNERMOST, ADD)
-        nc.sync.dma_start(out_rows, sums[:])
+        norms_from_stats(slice(0, LAST), slice(PICKED, ANCHOR + 1), slice(0, PIECES))
+        norms_from_stats(slice(LAST, BLOCKS), slice(ANCHOR, ANCHOR + 1), slice(0, PAIR))
+        nc.vector.tensor_reduce(sums[:, 0:FOLDED, DOT, :], folded[:], INNERMOST, ADD)
+        nc.vector.tensor_reduce(sums[:, FOLDED, DOT, 0:PAIR], folded_late[:], INNERMOST, ADD)
+        nc.sync.dma_start(out_rows, sums[:].rearrange("p n k b -> p n (k b)"))

@@ -41,7 +41,6 @@ def tile_ntxentlosschildrenfmapsclean_kernel(tc, x, anchor, offs, out):
         tc.psum_pool(name="banks", bufs=1) as banks,
     ):
         offsets = held.tile([PARTS, PIECES * OFFSET_COLUMNS], U16, name="offsets")
-        nc.sync.dma_start(offsets[:], offs)
 
         pairs = [(n, h) for n in range(BLOCKS) for h in range(PAIRS)]
         windows = {}
@@ -57,6 +56,8 @@ def tile_ntxentlosschildrenfmapsclean_kernel(tc, x, anchor, offs, out):
             for b in range(h * PAIR, (h + 1) * PAIR):
                 windows[n, b] = held.tile([PARTS, CHILDREN], F32, name=f"window{n}_{b}")
                 nc.sync.dma_start(windows[n, b][:], x_blocks[b, n])
+                if (n, b) == (0, 0):
+                    nc.sync.dma_start(offsets[:], offs)
             if n < LAST:
                 load_anchors(n, h)
 

@@ -91,11 +91,19 @@ def tile_ntxentlosschildrenfmapsclean_kernel(tc, x, anchor, offs, out):
                 stats[:, blocks, rows, pieces, 2], MULT, ADD,
             )
 
-        def sums_of_products(n, h):
+        def sums_of_products(n, first, pieces):
             nc.vector.tensor_reduce(
-                sums[:, n, DOT, h * PAIR : (h + 1) * PAIR],
-                products[n, h][:].rearrange("p (two s) -> p two s", two=PAIR),
+                sums[:, n, DOT, first : first + pieces],
+                products[n, first // PAIR][:].rearrange("p (k s) -> p k s", k=pieces),
                 INNERMOST, ADD,
+            )
+
+        def product_and_sum(n, b):
+            unkept = scratch.tile([PARTS, CHILDREN], F32, name="unkept")
+            nc.vector.scalar_tensor_tensor(
+                unkept[:], picked[n, b // PAIR][:, columns_of(b)], 1.0,
+                anchors[n, b // PAIR][:, columns_of(b)],
+                MULT, MULT, accum_out=sums[:, n, DOT, b : b + 1],
             )
 
         picked = {}
@@ -113,7 +121,15 @@ def tile_ntxentlosschildrenfmapsclean_kernel(tc, x, anchor, offs, out):
             if n < LAST or h == 0:
                 stats_of_pair(anchors, ANCHOR, n, h)
             previous, waiting = waiting, None
-            if (n, h) != pairs[-1]:
+            if (n, h) == (LAST, 0):
+                products[n, h] = held.tile([PARTS, CHILDREN], F32, name=f"products{n}_{h}")
+                nc.gpsimd.tensor_tensor(
+                    products[n, h][:], picked[n, h][:, columns_of(1)],
+                    anchors[n, h][:, columns_of(1)], MULT,
+                )
+                waiting = (n, 1, 1)
+                product_and_sum(n, 0)
+            if n < LAST:
                 products[n, h] = held.tile([PARTS, PAIR * CHILDREN], F32, name=f"products{n}_{h}")
                 nc.gpsimd.tensor_tensor(products[n, h][:], picked[n, h][:], anchors[n, h][:], MULT)
                 if n < FOLDED or (n, h) == (FOLDED, 0):
@@ -130,19 +146,14 @@ def tile_ntxentlosschildrenfmapsclean_kernel(tc, x, anchor, offs, out):
                             start=(c == 0), stop=(c == CHUNKS - 1),
                         )
                 else:
-                    waiting = (n, h)
+                    waiting = (n, h * PAIR, PAIR)
             if n < LAST:
                 stats_of_pair(picked, PICKED, n, h)
             if previous is not None:
                 sums_of_products(*previous)
 
         for b in range(PIECES - PAIR, PIECES):
-            unkept = scratch.tile([PARTS, CHILDREN], F32, name="unkept")
-            nc.vector.scalar_tensor_tensor(
-                unkept[:], picked[pairs[-1]][:, columns_of(b)], 1.0,
-                anchors[pairs[-1]][:, columns_of(b)],
-                MULT, MULT, accum_out=sums[:, LAST, DOT, b : b + 1],
-            )
+            product_and_sum(LAST, b)
 
         for kind, tiles, first in ((ANCHOR, anchors, PAIR), (PICKED, picked, 0)):
             for b in range(first, PIECES):

@@ -51,20 +51,20 @@ def tile_ntxentlosschildrenfmapsclean_kernel(tc, x, anchor, offs, out):
             nc.sync.dma_start(anchors[n, h][:], anchor_blocks[n, h])
 
         for n, h in pairs:
-            if n == LAST:
+            if n >= BLOCKS // 2:
                 load_anchors(n, h)
             for b in range(h * PAIR, (h + 1) * PAIR):
                 windows[n, b] = held.tile([PARTS, CHILDREN], F32, name=f"window{n}_{b}")
                 nc.sync.dma_start(windows[n, b][:], x_blocks[b, n])
                 if (n, b) == (0, 0):
                     nc.sync.dma_start(offsets[:], offs)
-            if n < LAST:
+            if n < BLOCKS // 2:
                 load_anchors(n, h)
 
         identity = held.tile([PARTS, PARTS], F32, name="identity")
         make_identity(nc, identity[:])
 
-        sums = held.tile([PARTS, BLOCKS, KINDS, PIECES], F32, name="sums")
+        sums = held.tile([PARTS, BLOCKS, KINDS, PIECES], F32, name="sums", tag=f"window{LAST}_0")
         stats = held.tile([PARTS, BLOCKS, len(NORMS), PIECES, STATS], F32, name="stats")
         mean_squares = held.tile([PARTS, BLOCKS, len(NORMS), PIECES], F32, name="mean_squares")
 

import concourse.mybir as mybir
from concourse.masks import make_identity

F32 = mybir.dt.float32
U16 = mybir.dt.uint16
MULT = mybir.AluOpType.mult
ADD = mybir.AluOpType.add
COPY = mybir.ActivationFunctionType.Copy
SQUARE = mybir.ActivationFunctionType.Square
INNERMOST = mybir.AxisListType.X

PARTS = 128
PIECES = 4
FEATURES = 512
CHILDREN = 256
BLOCKS = FEATURES // PARTS
LAST = BLOCKS - 1
OFFSET_COLUMNS = CHILDREN // 16
PAIR = 2
PAIRS = PIECES // PAIR
DOT, PICKED, ANCHOR = 0, 1, 2
KINDS = 3
NORMS = (PICKED, ANCHOR)
STATS = 3
BANK = 512
CHUNKS = 4
WIDTH = CHILDREN // CHUNKS
FOLDED = BANK // (PIECES * WIDTH)


def tile_ntxentlosschildrenfmapsclean_kernel(tc, x, anchor, offs, out):
    nc = tc.nc

    x_blocks = x.rearrange("b (p n) s -> b n p s", n=BLOCKS)
    anchor_blocks = anchor.rearrange("(p n) (h s) -> n h p s", n=BLOCKS, s=PAIR * CHILDREN)
    out_rows = out.rearrange("(p n) c -> p n c", n=BLOCKS)

    with (
        tc.tile_pool(name="held", bufs=1) as held,
        tc.tile_pool(name="scratch", bufs=2) as scratch,
        tc.psum_pool(name="banks", bufs=1) as banks,
    ):
        offsets = held.tile([PARTS, PIECES * OFFSET_COLUMNS], U16, name="offsets")

        pairs = [(n, h) for n in range(BLOCKS) for h in range(PAIRS)]
        windows = {}
        anchors = {}

        def load_anchors(n, h):
            anchors[n, h] = held.tile([PARTS, PAIR * CHILDREN], F32, name=f"anchor{n}_{h}")
            nc.sync.dma_start(anchors[n, h][:], anchor_blocks[n, h])

        for n, h in pairs:
            if n >= BLOCKS // 2:
                load_anchors(n, h)
            for b in range(h * PAIR, (h + 1) * PAIR):
                windows[n, b] = held.tile([PARTS, CHILDREN], F32, name=f"window{n}_{b}")
                nc.sync.dma_start(windows[n, b][:], x_blocks[b, n])
                if (n, b) == (0, 0):
                    nc.sync.dma_start(offsets[:], offs)
            if n < BLOCKS // 2:
                load_anchors(n, h)

        identity = held.tile([PARTS, PARTS], F32, name="identity")
        make_identity(nc, identity[:])

        sums = held.tile([PARTS, BLOCKS, KINDS, PIECES], F32, name="sums", tag=f"window{LAST}_0")
        stats = held.tile([PARTS, BLOCKS, len(NORMS), PIECES, STATS], F32, name="stats")
        mean_squares = held.tile([PARTS, BLOCKS, len(NORMS), PIECES], F32, name="mean_squares")

        warm = held.tile([PARTS, 1], F32, name="warm")
        nc.scalar.memzero(warm[:])

        def columns_of(b):
            return slice((b % PAIR) * CHILDREN, (b % PAIR + 1) * CHILDREN)

        def stats_of_pair(tiles, kind, n, h):
            nc.vector.bn_stats(
                stats[:, n, NORMS.index(kind), h * PAIR : (h + 1) * PAIR, :],
                tiles[n, h][:].rearrange("p (two s) -> p s two", two=PAIR),
            )

        def norms_from_stats(blocks, kinds, pieces):
            rows = slice(NORMS.index(kinds.start), NORMS.index(kinds.stop - 1) + 1)
            squares = mean_squares[:, blocks, rows, pieces]
            nc.vector.tensor_tensor(
                squares, stats[:, blocks, rows, pieces, 1], stats[:, blocks, rows, pieces, 1], MULT
            )
            nc.vector.scalar_tensor_tensor(
                sums[:, blocks, kinds, pieces], squares, float(CHILDREN),
                stats[:, blocks, rows, pieces, 2], MULT, ADD,
            )

        def sums_of_products(n, first, pieces):
            nc.vector.tensor_reduce(
                sums[:, n, DOT, first : first + pieces],
                products[n, first // PAIR][:].rearrange("p (k s) -> p k s", k=pieces),
                INNERMOST, ADD,
            )

        def product_and_sum(n, b):
            unkept = scratch.tile([PARTS, CHILDREN], F32, name="unkept")
            nc.vector.scalar_tensor_tensor(
                unkept[:], picked[n, b // PAIR][:, columns_of(b)], 1.0,
                anchors[n, b // PAIR][:, columns_of(b)],
                MULT, MULT, accum_out=sums[:, n, DOT, b : b + 1],
            )

        picked = {}
        products = {}
        folded = banks.tile([PARTS, FOLDED, PIECES, WIDTH], F32, name="folded")
        folded_late = banks.tile([PARTS, PAIR, WIDTH], F32, name="folded_late")
        waiting = None
        for n, h in pairs:
            picked[n, h] = held.tile([PARTS, PAIR * CHILDREN], F32, name=f"picked{n}_{h}")
            for b in range(h * PAIR, (h + 1) * PAIR):
                piece = offsets[:, b * OFFSET_COLUMNS : (b + 1) * OFFSET_COLUMNS]
                nc.scalar.activation(
                    picked[n, h][:, columns_of(b)], windows[n, b][:].indirect(piece), COPY
                )
            if n < LAST or h == 0:
                stats_of_pair(anchors, ANCHOR, n, h)
            previous, waiting = waiting, None
            if (n, h) == (LAST, 0):
                products[n, h] = held.tile([PARTS, CHILDREN], F32, name=f"products{n}_{h}")
                nc.gpsimd.tensor_tensor(
                    products[n, h][:], picked[n, h][:, columns_of(1)],
                    anchors[n, h][:, columns_of(1)], MULT,
                )
                waiting = (n, 1, 1)
                product_and_sum(n, 0)
            if n < LAST:
                products[n, h] = held.tile([PARTS, PAIR * CHILDREN], F32, name=f"products{n}_{h}")
                nc.gpsimd.tensor_tensor(products[n, h][:], picked[n, h][:], anchors[n, h][:], MULT)
                if n < FOLDED or (n, h) == (FOLDED, 0):
                    chunked = products[n, h][:].rearrange(
                        "p (two c w) -> p two c w", two=PAIR, c=CHUNKS
                    )
                    if n < FOLDED:
                        target = folded[:, n, h * PAIR : (h + 1) * PAIR, :]
                    else:
                        target = folded_late[:]
                    for c in range(CHUNKS):
                        nc.tensor.matmul(
                            target, identity[:], chunked[:, :, c, :],
                            start=(c == 0), stop=(c == CHUNKS - 1),
                        )
                else:
                    waiting = (n, h * PAIR, PAIR)
            if n < LAST:
                stats_of_pair(picked, PICKED, n, h)
            if previous is not None:
                sums_of_products(*previous)

        for b in range(PIECES - PAIR, PIECES):
            product_and_sum(LAST, b)

        for kind, tiles, first in ((ANCHOR, anchors, PAIR), (PICKED, picked, 0)):
            for b in range(first, PIECES):
                squares = scratch.tile([PARTS, CHILDREN], F32, name="squares")
                nc.scalar.activation(
                    squares[:], tiles[LAST, b // PAIR][:, columns_of(b)], SQUARE,
                    accum_out=sums[:, LAST, kind, b : b + 1],
                )

        norms_from_stats(slice(0, LAST), slice(PICKED, ANCHOR + 1), slice(0, PIECES))
        norms_from_stats(slice(LAST, BLOCKS), slice(ANCHOR, ANCHOR + 1), slice(0, PAIR))
        nc.vector.tensor_reduce(sums[:, 0:FOLDED, DOT, :], folded[:], INNERMOST, ADD)
        nc.vector.tensor_reduce(sums[:, FOLDED, DOT, 0:PAIR], folded_late[:], INNERMOST, ADD)
        nc.sync.dma_start(out_rows, sums[:].rearrange("p n k b -> p n (k b)"))
